import numpy as np
import ml_dtypes


def mxq(x, axis, fmt="e4m3"):
    dtype, down = {"e4m3": (ml_dtypes.float8_e4m3fn, 7), "e5m2": (ml_dtypes.float8_e5m2, 14)}[fmt]
    v = np.moveaxis(np.asarray(x, np.float32).astype(ml_dtypes.bfloat16).astype(np.float64), axis, -1)
    blocks = v.reshape(v.shape[:-1] + (-1, 32))
    amax = np.abs(blocks).max(-1, keepdims=True)
    byte = np.maximum(np.where(amax > 0, np.frexp(amax)[1] - 1 + 127, 0) - down, 1)
    scale = np.exp2(byte - 127.0)
    codes = (blocks / scale).astype(np.float32).astype(dtype).astype(np.float64)
    return np.moveaxis((codes * scale).reshape(v.shape), -1, axis)


WIDE = False


def mx_kscale(k):
    if not WIDE:
        return np.ones(k)
    levels = np.array([10, -10, 5, -5, 0])
    if k % 512:
        return np.exp2(np.random.permutation(np.resize(levels, k // 32))).repeat(32)
    a = np.empty((k // 512, 16))
    for p in range(k // 512):
        a[p, :8] = np.random.permutation(np.resize(levels, 8))
        for g in range(8):
            far = levels[np.abs(levels - a[p, g]) >= 10]
            a[p, g + 8] = far[np.random.randint(len(far))]
    return np.exp2(a.ravel()).repeat(32)


BF16 = ml_dtypes.bfloat16


def bf(x):
    return np.asarray(x, np.float32).astype(BF16)


def f64(x):
    return np.asarray(x).astype(np.float64)


B, IN, HID, OUT, LAYERS, NG = 1024, 512, 1024, 512, 2, 4
GW = NG * HID


def sigmoid(v):
    return 1.0 / (1.0 + np.exp(-v))


def setup_inputs():
    s = mx_kscale(IN)
    return {
        "regime_vector": bf(np.random.standard_normal((B, IN)) * s),
        "W_ih0": bf(np.random.standard_normal((GW, IN)) / np.sqrt(IN) / s),
        "hh_gates": bf(np.random.standard_normal(GW) * 0.5),
        "b_ih0": bf(np.random.standard_normal(GW) * 0.3),
        "b_hh0": bf(np.random.standard_normal(GW) * 0.3),
        "c_init": bf(np.random.standard_normal(HID)),
    }


def reference(regime_vector, W_ih0, hh_gates, b_ih0, b_hh0, c_init):
    gates = (mxq(f64(regime_vector), 1, "e4m3") @ mxq(f64(W_ih0).T, 0, "e4m3")) + f64(hh_gates) + (f64(b_ih0) + f64(b_hh0))
    i, f, g, o = np.split(gates, NG, axis=-1)
    i, f, o = sigmoid(i), sigmoid(f), sigmoid(o)
    g = np.tanh(g)
    c_new = f * f64(c_init) + i * g
    return o * np.tanh(c_new)

@@ -1,0 +1,282 @@
+from contextlib import ExitStack
+
+import concourse.mybir as mybir
+from concourse.masks import make_identity
+
+F32 = mybir.dt.float32
+BF16 = mybir.dt.bfloat16
+U32 = mybir.dt.uint32
+U8 = mybir.dt.uint8
+FP8X4 = mybir.dt.float8_e4m3fn_x4
+ACT = mybir.ActivationFunctionType
+ALU = mybir.AluOpType
+
+P = 128
+BATCH, K, HID, GATES = 1024, 512, 1024, 4
+PACK = 4
+BANK = 512
+PIECE = 2 * P
+X_PIECES = BATCH // PIECE
+W_PIECES = GATES * HID // PIECE
+HID_BLOCKS = HID // P
+HALVES = BATCH // BANK
+UNITS = HID_BLOCKS * HALVES
+GATE_I, GATE_F, GATE_G, GATE_O = 0, 1, 2, 3
+VECTOR_ROWS = GATES * HID // P
+LAST_UNIT_PARTS = 2
+
+FLOPS = 2 * BATCH * GATES * HID * K
+
+
+def tile_rdecommunicationlstm_pa_kernel(
+    tc, regime_vector, W_ih0, hh_gates, b_ih0, b_hh0, c_init, out
+):
+    nc = tc.nc
+    with ExitStack() as ctx:
+        const = ctx.enter_context(tc.tile_pool(name="const", bufs=1))
+        raw_pool = ctx.enter_context(tc.tile_pool(name="raw", bufs=X_PIECES + W_PIECES))
+        grouped_pool = ctx.enter_context(tc.tile_pool(name="grouped", bufs=4))
+        w_mx_pool = ctx.enter_context(tc.tile_pool(name="w_mx", bufs=W_PIECES))
+        cell_pool = ctx.enter_context(tc.tile_pool(name="cell", bufs=3))
+        psum = ctx.enter_context(tc.psum_pool(name="psum", bufs=1))
+        ctx.enter_context(tc.manual_schedule())
+
+        vector_rows = const.tile([P, P], BF16)
+        nc.vector.memset(vector_rows[:], 0.0)
+        for slot, vec in enumerate((hh_gates, b_ih0, b_hh0)):
+            nc.scalar.dma_start(
+                out=vector_rows[slot * VECTOR_ROWS : (slot + 1) * VECTOR_ROWS, :],
+                in_=vec.rearrange("(r c) -> r c", c=P),
+            )
+        nc.scalar.dma_start(
+            out=vector_rows[3 * VECTOR_ROWS : 3 * VECTOR_ROWS + HID_BLOCKS, :],
+            in_=c_init.rearrange("(r c) -> r c", c=P),
+        )
+
+        x_rows = regime_vector.rearrange("(c a p) k -> c p a k", a=2, p=P)
+        w_rows = W_ih0.rearrange("(h e j p) k -> j e p h k", h=2, e=2, p=P)
+
+        def load(rows):
+            raw = raw_pool.tile([P, 2 * K], BF16, tag="raw")
+            nc.sync.dma_start(out=raw[:].rearrange("p (a k) -> p a k", a=2), in_=rows)
+            return raw
+
+        raw_x = {}
+        raw_w = {}
+        for c in (0, 1):
+            raw_x[c] = load(x_rows[c])
+        for w in (0, 1):
+            raw_w[w] = load(w_rows[0, w])
+        for c in (2, 3):
+            raw_x[c] = load(x_rows[c])
+        for w in range(2, W_PIECES):
+            raw_w[w] = load(w_rows[w // 2, w % 2])
+
+        ident = const.tile([P, P], F32)
+        make_identity(nc, ident[:])
+        warm_in = const.tile([P, 1], F32)
+        warm_out = const.tile([P, 1], F32)
+        nc.vector.memset(warm_in[:], 0.0)
+        nc.scalar.activation(out=warm_out[:], in_=warm_in[:], func=ACT.Sigmoid)
+
+        x_codes = const.tile([P, BATCH], U32, align_bytes=64)
+        x_scales = const.tile([P, BATCH], U8, align_bytes=64)
+
+        def transpose_words(raw):
+            bank = psum.tile([P, BANK], F32, tag="work", bufs=5)
+            words = raw[:].bitcast(F32)
+            for s in range(BANK // P):
+                a, u = divmod(s, 2)
+                nc.tensor.transpose(
+                    out=bank[:, s * P : (s + 1) * P],
+                    in_=words[:, a * PIECE + u : (a + 1) * PIECE : 2],
+                    identity=ident[:],
+                )
+            return bank
+
+        def regroup(copy, bank):
+            grouped = grouped_pool.tile([P, PIECE * PACK], BF16, tag="grouped", align_bytes=64)
+            copy(
+                out=grouped[:].bitcast(F32).rearrange("p (a r u) -> p a r u", a=2, u=2),
+                in_=bank[:].rearrange("p (a u r) -> p a r u", a=2, u=2),
+            )
+            return grouped
+
+        def quantise(grouped, codes, scales):
+            nc.vector.quantize_mx(out=codes.bitcast(FP8X4), scales=scales, in_=grouped[:])
+
+        def quantise_x(c, grouped):
+            cols = slice(c * PIECE, (c + 1) * PIECE)
+            quantise(grouped, x_codes[:, cols], x_scales[:, cols])
+
+        w_mx = {}
+
+        def quantise_w(w, grouped):
+            w_codes = w_mx_pool.tile([P, PIECE], U32, tag="w_codes", align_bytes=64)
+            w_scales = w_mx_pool.tile([P, PIECE], U8, tag="w_scales", align_bytes=64)
+            quantise(grouped, w_codes[:], w_scales[:])
+            w_mx[w] = (w_codes, w_scales)
+
+        gate_bank = {}
+        cell = {}
+
+        def multiply(unit, e):
+            j, n = divmod(unit, HALVES)
+            w_codes, w_scales = w_mx[2 * j + e]
+            batch = slice(n * BANK, (n + 1) * BANK)
+            for h in range(2):
+                hidden = slice(h * P, (h + 1) * P)
+                bank = psum.tile([P, BANK], F32, tag="work", bufs=5)
+                nc.tensor.matmul_mx(
+                    out=bank[:],
+                    lhsT=w_codes[:, hidden].bitcast(FP8X4),
+                    lhsT_scale=w_scales[:, hidden],
+                    rhs=x_codes[:, batch].bitcast(FP8X4),
+                    rhs_scale=x_scales[:, batch],
+                    start=True,
+                    stop=True,
+                )
+                gate_bank[unit, 2 * h + e] = bank
+
+        def activate_gate(unit, gate, func, name):
+            j = unit // HALVES
+            col = gate * HID_BLOCKS + j
+            act = cell_pool.tile([P, BANK], F32, tag=name)
+            nc.scalar.activation(
+                out=act[:], in_=gate_bank[unit, gate][:], func=func, bias=bias[:, col : col + 1]
+            )
+            cell[unit, name] = act
+
+        def parts_of(unit):
+            parts = LAST_UNIT_PARTS if unit == UNITS - 1 else 1
+            width = BANK // parts
+            return [(k * width, (k + 1) * width) for k in range(parts)]
+
+        def input_times_candidate(unit):
+            ig = cell_pool.tile([P, BANK], F32, tag="ig")
+            for lo, hi in parts_of(unit):
+                nc.vector.tensor_tensor(
+                    out=ig[:, lo:hi],
+                    in0=cell[unit, "i"][:, lo:hi],
+                    in1=cell[unit, "g"][:, lo:hi],
+                    op=ALU.mult,
+                )
+            cell[unit, "ig"] = ig
+
+        def new_cell_state(unit):
+            j = unit // HALVES
+            c_new = cell_pool.tile([P, BANK], F32, tag="c_new")
+            for lo, hi in parts_of(unit):
+                nc.vector.scalar_tensor_tensor(
+                    out=c_new[:, lo:hi],
+                    in0=cell[unit, "f"][:, lo:hi],
+                    scalar=c_start[:, j : j + 1],
+                    in1=cell[unit, "ig"][:, lo:hi],
+                    op0=ALU.mult,
+                    op1=ALU.add,
+                )
+            cell[unit, "c_new"] = c_new
+
+        def batch_onto_partitions(unit, name, lo, hi):
+            bank = psum.tile([P, BANK], F32, tag="back", bufs=3)
+            for first in range(lo, hi, P):
+                block = slice(first, first + P)
+                nc.tensor.transpose(
+                    out=bank[:, block], in_=cell[unit, name][:, block], identity=ident[:]
+                )
+            return bank
+
+        def tanh_of_cell_state(unit):
+            tanh_c = cell_pool.tile([P, BANK], F32, tag="tanh_c")
+            for lo, hi in parts_of(unit):
+                nc.scalar.activation(
+                    out=tanh_c[:, lo:hi], in_=cell[unit, "c_T", lo][:, lo:hi], func=ACT.Tanh
+                )
+            cell[unit, "tanh_c"] = tanh_c
+
+        out_blocks = out.rearrange("(n t p) (j c) -> n j p t c", t=BANK // P, p=P, c=P)
+
+        def hidden_state(unit):
+            j, n = divmod(unit, HALVES)
+            h_new = cell_pool.tile([P, BANK], F32, tag="h_new")
+            for lo, hi in parts_of(unit):
+                nc.vector.tensor_tensor(
+                    out=h_new[:, lo:hi],
+                    in0=cell[unit, "o_T"][:, lo:hi],
+                    in1=cell[unit, "tanh_c"][:, lo:hi],
+                    op=ALU.mult,
+                )
+                nc.sync.dma_start(
+                    out=out_blocks[n, j, :, lo // P : hi // P, :],
+                    in_=h_new[:, lo:hi].rearrange("p (t c) -> p t c", c=P),
+                )
+
+        grouped_x = {}
+        grouped_w = {}
+        for c in (0, 1):
+            grouped_x[c] = regroup(nc.scalar.copy, transpose_words(raw_x[c]))
+
+        vector_rows_f32 = const.tile([P, P], F32)
+        nc.vector.tensor_copy(out=vector_rows_f32[:], in_=vector_rows[:])
+        vector_bank = psum.tile([P, BANK], F32, tag="work", bufs=5)
+        nc.tensor.transpose(out=vector_bank[:, 0:P], in_=vector_rows_f32[:], identity=ident[:])
+        vector_cols = const.tile([P, P], F32)
+        nc.vector.tensor_copy(out=vector_cols[:], in_=vector_bank[:, 0:P])
+        c_start = vector_cols[:, 3 * VECTOR_ROWS : 3 * VECTOR_ROWS + HID_BLOCKS]
+
+        for c in (0, 1):
+            quantise_x(c, grouped_x[c])
+        for w in (0, 1):
+            grouped_w[w] = regroup(nc.scalar.copy, transpose_words(raw_w[w]))
+        x_bank = {}
+        for c in (2, 3):
+            x_bank[c] = transpose_words(raw_x[c])
+        quantise_w(0, grouped_w[0])
+        multiply(0, 0)
+
+        bias_ih_hh = const.tile([P, VECTOR_ROWS], F32)
+        bias = const.tile([P, VECTOR_ROWS], F32)
+        nc.vector.tensor_tensor(
+            out=bias_ih_hh[:],
+            in0=vector_cols[:, VECTOR_ROWS : 2 * VECTOR_ROWS],
+            in1=vector_cols[:, 2 * VECTOR_ROWS : 3 * VECTOR_ROWS],
+            op=ALU.add,
+        )
+        grouped_x[2] = regroup(nc.vector.tensor_copy, x_bank[2])
+        nc.vector.tensor_tensor(
+            out=bias[:], in0=vector_cols[:, 0:VECTOR_ROWS], in1=bias_ih_hh[:], op=ALU.add
+        )
+        quantise_w(1, grouped_w[1])
+        multiply(0, 1)
+        grouped_x[3] = regroup(nc.vector.tensor_copy, x_bank[3])
+        quantise_x(2, grouped_x[2])
+        w_bank = {2: transpose_words(raw_w[2])}
+        quantise_x(3, grouped_x[3])
+        grouped_w[2] = regroup(nc.vector.tensor_copy, w_bank[2])
+
+        for t in range(UNITS + 1):
+            if t + 3 < W_PIECES:
+                w_bank[t + 3] = transpose_words(raw_w[t + 3])
+            if t < UNITS:
+                activate_gate(t, GATE_I, ACT.Sigmoid, "i")
+                activate_gate(t, GATE_G, ACT.Tanh, "g")
+                activate_gate(t, GATE_F, ACT.Sigmoid, "f")
+                activate_gate(t, GATE_O, ACT.Sigmoid, "o")
+            if t >= 1:
+                tanh_of_cell_state(t - 1)
+            if t < UNITS:
+                input_times_candidate(t)
+            if t + 2 < W_PIECES:
+                quantise_w(t + 2, grouped_w[t + 2])
+            if t + 1 < UNITS:
+                multiply(t + 1, 0)
+                multiply(t + 1, 1)
+            if t < UNITS:
+                new_cell_state(t)
+                for lo, hi in parts_of(t):
+                    cell[t, "c_T", lo] = batch_onto_partitions(t, "c_new", lo, hi)
+                cell[t, "o_T"] = batch_onto_partitions(t, "o", 0, BANK)
+            if t + 3 < W_PIECES:
+                grouped_w[t + 3] = regroup(nc.vector.tensor_copy, w_bank[t + 3])
+            if t >= 1:
+                hidden_state(t - 1)

@@ -37,7 +37,7 @@ def tile_rdecommunicationlstm_pa_kernel(
         raw_pool = ctx.enter_context(tc.tile_pool(name="raw", bufs=X_PIECES + W_PIECES))
         grouped_pool = ctx.enter_context(tc.tile_pool(name="grouped", bufs=4))
         w_mx_pool = ctx.enter_context(tc.tile_pool(name="w_mx", bufs=W_PIECES))
-        cell_pool = ctx.enter_context(tc.tile_pool(name="cell", bufs=3))
+        cell_pool = ctx.enter_context(tc.tile_pool(name="cell", bufs=4))
         psum = ctx.enter_context(tc.psum_pool(name="psum", bufs=1))
         ctx.enter_context(tc.manual_schedule())
 
@@ -63,10 +63,9 @@ def tile_rdecommunicationlstm_pa_kernel(
 
         raw_x = {}
         raw_w = {}
-        for c in (0, 1):
-            raw_x[c] = load(x_rows[c])
-        for w in (0, 1):
-            raw_w[w] = load(w_rows[0, w])
+        for piece in (0, 1):
+            raw_x[piece] = load(x_rows[piece])
+            raw_w[piece] = load(w_rows[0, piece])
         for c in (2, 3):
             raw_x[c] = load(x_rows[c])
         for w in range(2, W_PIECES):
@@ -79,11 +78,35 @@ def tile_rdecommunicationlstm_pa_kernel(
         nc.vector.memset(warm_in[:], 0.0)
         nc.scalar.activation(out=warm_out[:], in_=warm_in[:], func=ACT.Sigmoid)
 
+        select = const.tile([P, VECTOR_ROWS + HID_BLOCKS], BF16)
+        two_slots = const.tile([P, VECTOR_ROWS], F32)
+        nc.vector.tensor_tensor(
+            out=two_slots[:],
+            in0=ident[:, 0:VECTOR_ROWS],
+            in1=ident[:, VECTOR_ROWS : 2 * VECTOR_ROWS],
+            op=ALU.add,
+        )
+        nc.vector.tensor_copy(
+            out=select[:, VECTOR_ROWS : VECTOR_ROWS + HID_BLOCKS],
+            in_=ident[:, 3 * VECTOR_ROWS : 3 * VECTOR_ROWS + HID_BLOCKS],
+        )
+        nc.vector.tensor_tensor(
+            out=select[:, 0:VECTOR_ROWS],
+            in0=two_slots[:],
+            in1=ident[:, 2 * VECTOR_ROWS : 3 * VECTOR_ROWS],
+            op=ALU.add,
+        )
+
         x_codes = const.tile([P, BATCH], U32, align_bytes=64)
         x_scales = const.tile([P, BATCH], U8, align_bytes=64)
 
-        def transpose_words(raw):
-            bank = psum.tile([P, BANK], F32, tag="work", bufs=5)
+        def work_bank():
+            return psum.tile([P, BANK], F32, tag="work", bufs=5, name="work")
+
+        def back_bank():
+            return psum.tile([P, BANK], F32, tag="back", bufs=3, name="back")
+
+        def transpose_words(raw, bank):
             words = raw[:].bitcast(F32)
             for s in range(BANK // P):
                 a, u = divmod(s, 2)
@@ -120,15 +143,15 @@ def tile_rdecommunicationlstm_pa_kernel(
         gate_bank = {}
         cell = {}
 
-        def multiply(unit, e):
+        def multiply(unit, e, lo=0, hi=BANK):
             j, n = divmod(unit, HALVES)
             w_codes, w_scales = w_mx[2 * j + e]
-            batch = slice(n * BANK, (n + 1) * BANK)
+            batch = slice(n * BANK + lo, n * BANK + hi)
             for h in range(2):
                 hidden = slice(h * P, (h + 1) * P)
-                bank = psum.tile([P, BANK], F32, tag="work", bufs=5)
+                bank = work_bank()
                 nc.tensor.matmul_mx(
-                    out=bank[:],
+                    out=bank[:, lo:hi],
                     lhsT=w_codes[:, hidden].bitcast(FP8X4),
                     lhsT_scale=w_scales[:, hidden],
                     rhs=x_codes[:, batch].bitcast(FP8X4),
@@ -136,16 +159,19 @@ def tile_rdecommunicationlstm_pa_kernel(
                     start=True,
                     stop=True,
                 )
-                gate_bank[unit, 2 * h + e] = bank
+                gate_bank[unit, 2 * h + e, lo] = bank
 
-        def activate_gate(unit, gate, func, name):
+        def activate_gate(unit, gate, func, name, lo=0, hi=BANK):
             j = unit // HALVES
             col = gate * HID_BLOCKS + j
-            act = cell_pool.tile([P, BANK], F32, tag=name)
+            if lo == 0:
+                cell[unit, name] = cell_pool.tile([P, BANK], F32, tag=name, name=name)
             nc.scalar.activation(
-                out=act[:], in_=gate_bank[unit, gate][:], func=func, bias=bias[:, col : col + 1]
+                out=cell[unit, name][:, lo:hi],
+                in_=gate_bank[unit, gate, lo][:, lo:hi],
+                func=func,
+                bias=vector_cols[:, col : col + 1],
             )
-            cell[unit, name] = act
 
         def parts_of(unit):
             parts = LAST_UNIT_PARTS if unit == UNITS - 1 else 1
@@ -170,21 +196,26 @@ def tile_rdecommunicationlstm_pa_kernel(
                 nc.vector.scalar_tensor_tensor(
                     out=c_new[:, lo:hi],
                     in0=cell[unit, "f"][:, lo:hi],
-                    scalar=c_start[:, j : j + 1],
+                    scalar=vector_cols[:, VECTOR_ROWS + j : VECTOR_ROWS + j + 1],
                     in1=cell[unit, "ig"][:, lo:hi],
                     op0=ALU.mult,
                     op1=ALU.add,
                 )
             cell[unit, "c_new"] = c_new
 
-        def batch_onto_partitions(unit, name, lo, hi):
-            bank = psum.tile([P, BANK], F32, tag="back", bufs=3)
+        def batch_onto_partitions(unit, name, lo, hi, bank):
             for first in range(lo, hi, P):
                 block = slice(first, first + P)
                 nc.tensor.transpose(
                     out=bank[:, block], in_=cell[unit, name][:, block], identity=ident[:]
                 )
             return bank
+
+        def way_back(unit):
+            for lo, hi in parts_of(unit):
+                cell[unit, "c_T", lo] = batch_onto_partitions(unit, "c_new", lo, hi, back_bank())
+            bank = work_bank() if unit == UNITS - 1 else back_bank()
+            cell[unit, "o_T"] = batch_onto_partitions(unit, "o", 0, BANK, bank)
 
         def tanh_of_cell_state(unit):
             tanh_c = cell_pool.tile([P, BANK], F32, tag="tanh_c")
@@ -213,70 +244,97 @@ def tile_rdecommunicationlstm_pa_kernel(
 
         grouped_x = {}
         grouped_w = {}
-        for c in (0, 1):
-            grouped_x[c] = regroup(nc.scalar.copy, transpose_words(raw_x[c]))
-
-        vector_rows_f32 = const.tile([P, P], F32)
-        nc.vector.tensor_copy(out=vector_rows_f32[:], in_=vector_rows[:])
-        vector_bank = psum.tile([P, BANK], F32, tag="work", bufs=5)
-        nc.tensor.transpose(out=vector_bank[:, 0:P], in_=vector_rows_f32[:], identity=ident[:])
-        vector_cols = const.tile([P, P], F32)
-        nc.vector.tensor_copy(out=vector_cols[:], in_=vector_bank[:, 0:P])
-        c_start = vector_cols[:, 3 * VECTOR_ROWS : 3 * VECTOR_ROWS + HID_BLOCKS]
-
-        for c in (0, 1):
-            quantise_x(c, grouped_x[c])
-        for w in (0, 1):
-            grouped_w[w] = regroup(nc.scalar.copy, transpose_words(raw_w[w]))
         x_bank = {}
-        for c in (2, 3):
-            x_bank[c] = transpose_words(raw_x[c])
-        quantise_w(0, grouped_w[0])
-        multiply(0, 0)
+        w_bank = {}
+        HALF = BANK // 2
 
-        bias_ih_hh = const.tile([P, VECTOR_ROWS], F32)
-        bias = const.tile([P, VECTOR_ROWS], F32)
-        nc.vector.tensor_tensor(
-            out=bias_ih_hh[:],
-            in0=vector_cols[:, VECTOR_ROWS : 2 * VECTOR_ROWS],
-            in1=vector_cols[:, 2 * VECTOR_ROWS : 3 * VECTOR_ROWS],
-            op=ALU.add,
+        def input_and_candidate(unit, lo, hi):
+            multiply(unit, 0, lo, hi)
+            activate_gate(unit, GATE_I, ACT.Sigmoid, "i", lo, hi)
+            activate_gate(unit, GATE_G, ACT.Tanh, "g", lo, hi)
+
+        x_bank[0] = transpose_words(raw_x[0], work_bank())
+        grouped_x[0] = regroup(nc.scalar.copy, x_bank[0])
+        w_bank[0] = transpose_words(raw_w[0], work_bank())
+        grouped_w[0] = regroup(nc.scalar.copy, w_bank[0])
+        quantise_x(0, grouped_x[0])
+        x_bank[1] = transpose_words(raw_x[1], work_bank())
+        grouped_x[1] = regroup(nc.scalar.copy, x_bank[1])
+        quantise_w(0, grouped_w[0])
+        w_bank[1] = transpose_words(raw_w[1], work_bank())
+        grouped_w[1] = regroup(nc.scalar.copy, w_bank[1])
+
+        vector_bank = back_bank()
+        nc.tensor.matmul(
+            out=vector_bank[:, 0 : VECTOR_ROWS + HID_BLOCKS],
+            lhsT=vector_rows[:],
+            rhs=select[:],
+            start=True,
+            stop=True,
         )
-        grouped_x[2] = regroup(nc.vector.tensor_copy, x_bank[2])
-        nc.vector.tensor_tensor(
-            out=bias[:], in0=vector_cols[:, 0:VECTOR_ROWS], in1=bias_ih_hh[:], op=ALU.add
-        )
+        vector_cols = const.tile([P, VECTOR_ROWS + HID_BLOCKS], F32)
+        nc.vector.tensor_copy(out=vector_cols[:], in_=vector_bank[:, 0 : VECTOR_ROWS + HID_BLOCKS])
+
+        x_bank[2] = transpose_words(raw_x[2], back_bank())
+        input_and_candidate(0, 0, HALF)
+        quantise_x(1, grouped_x[1])
+        input_and_candidate(0, HALF, BANK)
+        x_bank[3] = transpose_words(raw_x[3], back_bank())
         quantise_w(1, grouped_w[1])
         multiply(0, 1)
-        grouped_x[3] = regroup(nc.vector.tensor_copy, x_bank[3])
+        activate_gate(0, GATE_F, ACT.Sigmoid, "f")
+        activate_gate(0, GATE_O, ACT.Sigmoid, "o")
+        w_bank[2] = transpose_words(raw_w[2], back_bank())
+        grouped_x[2] = regroup(nc.vector.tensor_copy, x_bank[2])
         quantise_x(2, grouped_x[2])
-        w_bank = {2: transpose_words(raw_w[2])}
+        input_and_candidate(1, 0, HALF)
+        grouped_w[2] = regroup(nc.scalar.copy, w_bank[2])
+        grouped_x[3] = regroup(nc.vector.tensor_copy, x_bank[3])
         quantise_x(3, grouped_x[3])
-        grouped_w[2] = regroup(nc.vector.tensor_copy, w_bank[2])
+        input_and_candidate(1, HALF, BANK)
+        multiply(1, 1)
+        activate_gate(1, GATE_F, ACT.Sigmoid, "f")
+        activate_gate(1, GATE_O, ACT.Sigmoid, "o")
+        input_times_candidate(0)
+        quantise_w(2, grouped_w[2])
+        new_cell_state(0)
+        w_bank[3] = transpose_words(raw_w[3], back_bank())
+        multiply(2, 0)
+        way_back(0)
+        grouped_w[3] = regroup(nc.vector.tensor_copy, w_bank[3])
+        w_bank[4] = transpose_words(raw_w[4], work_bank())
+        input_times_candidate(1)
+        quantise_w(3, grouped_w[3])
+        new_cell_state(1)
+        multiply(2, 1)
+        grouped_w[4] = regroup(nc.vector.tensor_copy, w_bank[4])
+        way_back(1)
 
-        for t in range(UNITS + 1):
+        for t in range(2, UNITS):
             if t + 3 < W_PIECES:
-                w_bank[t + 3] = transpose_words(raw_w[t + 3])
-            if t < UNITS:
-                activate_gate(t, GATE_I, ACT.Sigmoid, "i")
-                activate_gate(t, GATE_G, ACT.Tanh, "g")
-                activate_gate(t, GATE_F, ACT.Sigmoid, "f")
-                activate_gate(t, GATE_O, ACT.Sigmoid, "o")
-            if t >= 1:
+                w_bank[t + 3] = transpose_words(raw_w[t + 3], work_bank())
+            activate_gate(t, GATE_I, ACT.Sigmoid, "i")
+            activate_gate(t, GATE_G, ACT.Tanh, "g")
+            if t == 2:
+                tanh_of_cell_state(0)
+            activate_gate(t, GATE_F, ACT.Sigmoid, "f")
+            if t == UNITS - 1:
                 tanh_of_cell_state(t - 1)
-            if t < UNITS:
-                input_times_candidate(t)
+            activate_gate(t, GATE_O, ACT.Sigmoid, "o")
+            if t < UNITS - 1:
+                tanh_of_cell_state(t - 1)
+            if t == 2:
+                hidden_state(0)
+            input_times_candidate(t)
             if t + 2 < W_PIECES:
                 quantise_w(t + 2, grouped_w[t + 2])
             if t + 1 < UNITS:
                 multiply(t + 1, 0)
                 multiply(t + 1, 1)
-            if t < UNITS:
-                new_cell_state(t)
-                for lo, hi in parts_of(t):
-                    cell[t, "c_T", lo] = batch_onto_partitions(t, "c_new", lo, hi)
-                cell[t, "o_T"] = batch_onto_partitions(t, "o", 0, BANK)
+            new_cell_state(t)
+            way_back(t)
             if t + 3 < W_PIECES:
                 grouped_w[t + 3] = regroup(nc.vector.tensor_copy, w_bank[t + 3])
-            if t >= 1:
-                hidden_state(t - 1)
+            hidden_state(t - 1)
+        tanh_of_cell_state(UNITS - 1)
+        hidden_state(UNITS - 1)

@@ -311,8 +311,6 @@ def tile_rdecommunicationlstm_pa_kernel(
         way_back(1)
 
         for t in range(2, UNITS):
-            if t + 3 < W_PIECES:
-                w_bank[t + 3] = transpose_words(raw_w[t + 3], work_bank())
             activate_gate(t, GATE_I, ACT.Sigmoid, "i")
             activate_gate(t, GATE_G, ACT.Tanh, "g")
             if t == 2:
@@ -330,6 +328,9 @@ def tile_rdecommunicationlstm_pa_kernel(
                 quantise_w(t + 2, grouped_w[t + 2])
             if t + 1 < UNITS:
                 multiply(t + 1, 0)
+            if t + 3 < W_PIECES:
+                w_bank[t + 3] = transpose_words(raw_w[t + 3], work_bank())
+            if t + 1 < UNITS:
                 multiply(t + 1, 1)
             new_cell_state(t)
             way_back(t)

@@ -42,16 +42,14 @@ def tile_rdecommunicationlstm_pa_kernel(
         ctx.enter_context(tc.manual_schedule())
 
         vector_rows = const.tile([P, P], BF16)
-        nc.vector.memset(vector_rows[:], 0.0)
+        nc.vector.memset(vector_rows[3 * VECTOR_ROWS : P, :], 0.0)
+        c_rows = const.tile([P, P], BF16)
+        nc.vector.memset(c_rows[:], 0.0)
         for slot, vec in enumerate((hh_gates, b_ih0, b_hh0)):
             nc.scalar.dma_start(
                 out=vector_rows[slot * VECTOR_ROWS : (slot + 1) * VECTOR_ROWS, :],
                 in_=vec.rearrange("(r c) -> r c", c=P),
             )
-        nc.scalar.dma_start(
-            out=vector_rows[3 * VECTOR_ROWS : 3 * VECTOR_ROWS + HID_BLOCKS, :],
-            in_=c_init.rearrange("(r c) -> r c", c=P),
-        )
 
         x_rows = regime_vector.rearrange("(c a p) k -> c p a k", a=2, p=P)
         w_rows = W_ih0.rearrange("(h e j p) k -> j e p h k", h=2, e=2, p=P)
@@ -68,6 +66,7 @@ def tile_rdecommunicationlstm_pa_kernel(
             raw_w[piece] = load(w_rows[0, piece])
         for c in (2, 3):
             raw_x[c] = load(x_rows[c])
+        nc.sync.dma_start(out=c_rows[0:HID_BLOCKS, :], in_=c_init.rearrange("(r c) -> r c", c=P))
         for w in range(2, W_PIECES):
             raw_w[w] = load(w_rows[w // 2, w % 2])
 
@@ -78,7 +77,8 @@ def tile_rdecommunicationlstm_pa_kernel(
         nc.vector.memset(warm_in[:], 0.0)
         nc.scalar.activation(out=warm_out[:], in_=warm_in[:], func=ACT.Sigmoid)
 
-        select = const.tile([P, VECTOR_ROWS + HID_BLOCKS], BF16)
+        select = const.tile([P, VECTOR_ROWS], BF16)
+        first_rows = const.tile([P, HID_BLOCKS], BF16)
         two_slots = const.tile([P, VECTOR_ROWS], F32)
         nc.vector.tensor_tensor(
             out=two_slots[:],
@@ -86,12 +86,9 @@ def tile_rdecommunicationlstm_pa_kernel(
             in1=ident[:, VECTOR_ROWS : 2 * VECTOR_ROWS],
             op=ALU.add,
         )
-        nc.vector.tensor_copy(
-            out=select[:, VECTOR_ROWS : VECTOR_ROWS + HID_BLOCKS],
-            in_=ident[:, 3 * VECTOR_ROWS : 3 * VECTOR_ROWS + HID_BLOCKS],
-        )
+        nc.vector.tensor_copy(out=first_rows[:], in_=ident[:, 0:HID_BLOCKS])
         nc.vector.tensor_tensor(
-            out=select[:, 0:VECTOR_ROWS],
+            out=select[:],
             in0=two_slots[:],
             in1=ident[:, 2 * VECTOR_ROWS : 3 * VECTOR_ROWS],
             op=ALU.add,
@@ -170,7 +167,7 @@ def tile_rdecommunicationlstm_pa_kernel(
                 out=cell[unit, name][:, lo:hi],
                 in_=gate_bank[unit, gate, lo][:, lo:hi],
                 func=func,
-                bias=vector_cols[:, col : col + 1],
+                bias=bias[:, col : col + 1],
             )
 
         def parts_of(unit):
@@ -196,7 +193,7 @@ def tile_rdecommunicationlstm_pa_kernel(
                 nc.vector.scalar_tensor_tensor(
                     out=c_new[:, lo:hi],
                     in0=cell[unit, "f"][:, lo:hi],
-                    scalar=vector_cols[:, VECTOR_ROWS + j : VECTOR_ROWS + j + 1],
+                    scalar=c_start[:, j : j + 1],
                     in1=cell[unit, "ig"][:, lo:hi],
                     op0=ALU.mult,
                     op1=ALU.add,
@@ -264,16 +261,16 @@ def tile_rdecommunicationlstm_pa_kernel(
         w_bank[1] = transpose_words(raw_w[1], work_bank())
         grouped_w[1] = regroup(nc.scalar.copy, w_bank[1])
 
-        vector_bank = back_bank()
-        nc.tensor.matmul(
-            out=vector_bank[:, 0 : VECTOR_ROWS + HID_BLOCKS],
-            lhsT=vector_rows[:],
-            rhs=select[:],
-            start=True,
-            stop=True,
-        )
-        vector_cols = const.tile([P, VECTOR_ROWS + HID_BLOCKS], F32)
-        nc.vector.tensor_copy(out=vector_cols[:], in_=vector_bank[:, 0 : VECTOR_ROWS + HID_BLOCKS])
+        def sum_of_rows(rows, which, columns):
+            bank = back_bank()
+            nc.tensor.matmul(
+                out=bank[:, 0:columns], lhsT=rows[:], rhs=which[:], start=True, stop=True
+            )
+            return bank
+
+        bias_bank = sum_of_rows(vector_rows, select, VECTOR_ROWS)
+        bias = const.tile([P, VECTOR_ROWS], F32)
+        nc.vector.tensor_copy(out=bias[:], in_=bias_bank[:, 0:VECTOR_ROWS])
 
         x_bank[2] = transpose_words(raw_x[2], back_bank())
         input_and_candidate(0, 0, HALF)
@@ -285,6 +282,7 @@ def tile_rdecommunicationlstm_pa_kernel(
         activate_gate(0, GATE_F, ACT.Sigmoid, "f")
         activate_gate(0, GATE_O, ACT.Sigmoid, "o")
         w_bank[2] = transpose_words(raw_w[2], back_bank())
+        c_bank = sum_of_rows(c_rows, first_rows, HID_BLOCKS)
         grouped_x[2] = regroup(nc.vector.tensor_copy, x_bank[2])
         quantise_x(2, grouped_x[2])
         input_and_candidate(1, 0, HALF)
@@ -295,6 +293,8 @@ def tile_rdecommunicationlstm_pa_kernel(
         multiply(1, 1)
         activate_gate(1, GATE_F, ACT.Sigmoid, "f")
         activate_gate(1, GATE_O, ACT.Sigmoid, "o")
+        c_start = const.tile([P, HID_BLOCKS], F32)
+        nc.vector.tensor_copy(out=c_start[:], in_=c_bank[:, 0:HID_BLOCKS])
         input_times_candidate(0)
         quantise_w(2, grouped_w[2])
         new_cell_state(0)

@@ -70,6 +70,8 @@ def tile_rdecommunicationlstm_pa_kernel(
         for w in range(2, W_PIECES):
             raw_w[w] = load(w_rows[w // 2, w % 2])
 
+        zeros = const.tile([P, BANK], BF16)
+        nc.vector.memset(zeros[:], 0.0)
         ident = const.tile([P, P], F32)
         make_identity(nc, ident[:])
         warm_in = const.tile([P, 1], F32)
@@ -250,15 +252,27 @@ def tile_rdecommunicationlstm_pa_kernel(
             activate_gate(unit, GATE_I, ACT.Sigmoid, "i", lo, hi)
             activate_gate(unit, GATE_G, ACT.Tanh, "g", lo, hi)
 
+        def keep_clock_up(bank, times):
+            for i in range(times):
+                nc.tensor.matmul(
+                    out=bank[:], lhsT=zeros[:, 0:P], rhs=zeros[:], start=True, stop=True
+                )
+
+        idle_bank = back_bank()
+        keep_clock_up(idle_bank, 4)
         x_bank[0] = transpose_words(raw_x[0], work_bank())
+        keep_clock_up(idle_bank, 1)
         grouped_x[0] = regroup(nc.scalar.copy, x_bank[0])
         w_bank[0] = transpose_words(raw_w[0], work_bank())
+        keep_clock_up(idle_bank, 1)
         grouped_w[0] = regroup(nc.scalar.copy, w_bank[0])
         quantise_x(0, grouped_x[0])
         x_bank[1] = transpose_words(raw_x[1], work_bank())
+        keep_clock_up(idle_bank, 1)
         grouped_x[1] = regroup(nc.scalar.copy, x_bank[1])
         quantise_w(0, grouped_w[0])
         w_bank[1] = transpose_words(raw_w[1], work_bank())
+        keep_clock_up(idle_bank, 1)
         grouped_w[1] = regroup(nc.scalar.copy, w_bank[1])
 
         def sum_of_rows(rows, which, columns):

@@ -23,7 +23,8 @@ HALVES = BATCH // BANK
 UNITS = HID_BLOCKS * HALVES
 GATE_I, GATE_F, GATE_G, GATE_O = 0, 1, 2, 3
 VECTOR_ROWS = GATES * HID // P
-LAST_UNIT_PARTS = 2
+HALF = BANK // 2
+LAST_UNIT_PARTS = (2 * P, P, P)
 
 FLOPS = 2 * BATCH * GATES * HID * K
 
@@ -41,6 +42,8 @@ def tile_rdecommunicationlstm_pa_kernel(
         psum = ctx.enter_context(tc.psum_pool(name="psum", bufs=1))
         ctx.enter_context(tc.manual_schedule())
 
+        zeros = const.tile([P, P], BF16)
+        nc.vector.memset(zeros[:], 0.0)
         vector_rows = const.tile([P, P], BF16)
         nc.vector.memset(vector_rows[3 * VECTOR_ROWS : P, :], 0.0)
         c_rows = const.tile([P, P], BF16)
@@ -70,8 +73,6 @@ def tile_rdecommunicationlstm_pa_kernel(
         for w in range(2, W_PIECES):
             raw_w[w] = load(w_rows[w // 2, w % 2])
 
-        zeros = const.tile([P, BANK], BF16)
-        nc.vector.memset(zeros[:], 0.0)
         ident = const.tile([P, P], F32)
         make_identity(nc, ident[:])
         warm_in = const.tile([P, 1], F32)
@@ -167,19 +168,25 @@ def tile_rdecommunicationlstm_pa_kernel(
                 cell[unit, name] = cell_pool.tile([P, BANK], F32, tag=name, name=name)
             nc.scalar.activation(
                 out=cell[unit, name][:, lo:hi],
-                in_=gate_bank[unit, gate, lo][:, lo:hi],
+                in_=gate_bank[unit, gate, lo if (unit, gate, lo) in gate_bank else 0][:, lo:hi],
                 func=func,
                 bias=bias[:, col : col + 1],
             )
 
         def parts_of(unit):
-            parts = LAST_UNIT_PARTS if unit == UNITS - 1 else 1
-            width = BANK // parts
-            return [(k * width, (k + 1) * width) for k in range(parts)]
+            parts = []
+            lo = 0
+            for width in LAST_UNIT_PARTS if unit == UNITS - 1 else (BANK,):
+                parts.append((lo, lo + width))
+                lo += width
+            return parts
+
+        def halves_of(unit):
+            return [(0, HALF), (HALF, BANK)] if unit == UNITS - 1 else [(0, BANK)]
 
         def input_times_candidate(unit):
             ig = cell_pool.tile([P, BANK], F32, tag="ig")
-            for lo, hi in parts_of(unit):
+            for lo, hi in halves_of(unit):
                 nc.vector.tensor_tensor(
                     out=ig[:, lo:hi],
                     in0=cell[unit, "i"][:, lo:hi],
@@ -211,10 +218,11 @@ def tile_rdecommunicationlstm_pa_kernel(
             return bank
 
         def way_back(unit):
+            bank = work_bank if unit == UNITS - 1 else back_bank
             for lo, hi in parts_of(unit):
-                cell[unit, "c_T", lo] = batch_onto_partitions(unit, "c_new", lo, hi, back_bank())
-            bank = work_bank() if unit == UNITS - 1 else back_bank()
-            cell[unit, "o_T"] = batch_onto_partitions(unit, "o", 0, BANK, bank)
+                cell[unit, "c_T", lo] = batch_onto_partitions(unit, "c_new", lo, hi, bank())
+            for lo, hi in halves_of(unit):
+                cell[unit, "o_T", lo] = batch_onto_partitions(unit, "o", lo, hi, bank())
 
         def tanh_of_cell_state(unit):
             tanh_c = cell_pool.tile([P, BANK], F32, tag="tanh_c")
@@ -230,9 +238,10 @@ def tile_rdecommunicationlstm_pa_kernel(
             j, n = divmod(unit, HALVES)
             h_new = cell_pool.tile([P, BANK], F32, tag="h_new")
             for lo, hi in parts_of(unit):
+                half = max(start for start, stop in halves_of(unit) if start <= lo)
                 nc.vector.tensor_tensor(
                     out=h_new[:, lo:hi],
-                    in0=cell[unit, "o_T"][:, lo:hi],
+                    in0=cell[unit, "o_T", half][:, lo:hi],
                     in1=cell[unit, "tanh_c"][:, lo:hi],
                     op=ALU.mult,
                 )
@@ -245,34 +254,29 @@ def tile_rdecommunicationlstm_pa_kernel(
         grouped_w = {}
         x_bank = {}
         w_bank = {}
-        HALF = BANK // 2
 
         def input_and_candidate(unit, lo, hi):
             multiply(unit, 0, lo, hi)
             activate_gate(unit, GATE_I, ACT.Sigmoid, "i", lo, hi)
             activate_gate(unit, GATE_G, ACT.Tanh, "g", lo, hi)
 
-        def keep_clock_up(bank, times):
+        def keep_clock_up(times):
             for i in range(times):
                 nc.tensor.matmul(
-                    out=bank[:], lhsT=zeros[:, 0:P], rhs=zeros[:], start=True, stop=True
+                    out=idle_bank[:, 0:P], lhsT=zeros[:], rhs=zeros[:], start=True, stop=True
                 )
 
         idle_bank = back_bank()
-        keep_clock_up(idle_bank, 4)
+        keep_clock_up(12)
         x_bank[0] = transpose_words(raw_x[0], work_bank())
-        keep_clock_up(idle_bank, 1)
         grouped_x[0] = regroup(nc.scalar.copy, x_bank[0])
         w_bank[0] = transpose_words(raw_w[0], work_bank())
-        keep_clock_up(idle_bank, 1)
         grouped_w[0] = regroup(nc.scalar.copy, w_bank[0])
         quantise_x(0, grouped_x[0])
         x_bank[1] = transpose_words(raw_x[1], work_bank())
-        keep_clock_up(idle_bank, 1)
         grouped_x[1] = regroup(nc.scalar.copy, x_bank[1])
         quantise_w(0, grouped_w[0])
         w_bank[1] = transpose_words(raw_w[1], work_bank())
-        keep_clock_up(idle_bank, 1)
         grouped_w[1] = regroup(nc.scalar.copy, w_bank[1])
 
         def sum_of_rows(rows, which, columns):
@@ -300,7 +304,6 @@ def tile_rdecommunicationlstm_pa_kernel(
         grouped_x[2] = regroup(nc.vector.tensor_copy, x_bank[2])
         quantise_x(2, grouped_x[2])
         input_and_candidate(1, 0, HALF)
-        grouped_w[2] = regroup(nc.scalar.copy, w_bank[2])
         grouped_x[3] = regroup(nc.vector.tensor_copy, x_bank[3])
         quantise_x(3, grouped_x[3])
         input_and_candidate(1, HALF, BANK)
@@ -310,8 +313,9 @@ def tile_rdecommunicationlstm_pa_kernel(
         c_start = const.tile([P, HID_BLOCKS], F32)
         nc.vector.tensor_copy(out=c_start[:], in_=c_bank[:, 0:HID_BLOCKS])
         input_times_candidate(0)
-        quantise_w(2, grouped_w[2])
+        grouped_w[2] = regroup(nc.vector.tensor_copy, w_bank[2])
         new_cell_state(0)
+        quantise_w(2, grouped_w[2])
         w_bank[3] = transpose_words(raw_w[3], back_bank())
         multiply(2, 0)
         way_back(0)
@@ -332,7 +336,8 @@ def tile_rdecommunicationlstm_pa_kernel(
             activate_gate(t, GATE_F, ACT.Sigmoid, "f")
             if t == UNITS - 1:
                 tanh_of_cell_state(t - 1)
-            activate_gate(t, GATE_O, ACT.Sigmoid, "o")
+            for lo, hi in halves_of(t):
+                activate_gate(t, GATE_O, ACT.Sigmoid, "o", lo, hi)
             if t < UNITS - 1:
                 tanh_of_cell_state(t - 1)
             if t == 2:

@@ -54,7 +54,9 @@ def tile_rdecommunicationlstm_pa_kernel(
                 in_=vec.rearrange("(r c) -> r c", c=P),
             )
 
-        x_rows = regime_vector.rearrange("(c a p) k -> c p a k", a=2, p=P)
+        nc.scalar.dma_start(out=c_rows[0:HID_BLOCKS, :], in_=c_init.rearrange("(r c) -> r c", c=P))
+
+        x_rows = regime_vector.rearrange("(n p c a) k -> n c p a k", n=HALVES, p=P, a=2)
         w_rows = W_ih0.rearrange("(h e j p) k -> j e p h k", h=2, e=2, p=P)
 
         def load(rows):
@@ -65,11 +67,10 @@ def tile_rdecommunicationlstm_pa_kernel(
         raw_x = {}
         raw_w = {}
         for piece in (0, 1):
-            raw_x[piece] = load(x_rows[piece])
+            raw_x[piece] = load(x_rows[piece // 2, piece % 2])
             raw_w[piece] = load(w_rows[0, piece])
         for c in (2, 3):
-            raw_x[c] = load(x_rows[c])
-        nc.sync.dma_start(out=c_rows[0:HID_BLOCKS, :], in_=c_init.rearrange("(r c) -> r c", c=P))
+            raw_x[c] = load(x_rows[c // 2, c % 2])
         for w in range(2, W_PIECES):
             raw_w[w] = load(w_rows[w // 2, w % 2])
 
@@ -232,7 +233,7 @@ def tile_rdecommunicationlstm_pa_kernel(
                 )
             cell[unit, "tanh_c"] = tanh_c
 
-        out_blocks = out.rearrange("(n t p) (j c) -> n j p t c", t=BANK // P, p=P, c=P)
+        out_blocks = out.rearrange("(n p t) (j c) -> n j p t c", t=BANK // P, p=P, c=P)
 
         def hidden_state(unit):
             j, n = divmod(unit, HALVES)
@@ -294,24 +295,24 @@ def tile_rdecommunicationlstm_pa_kernel(
         input_and_candidate(0, 0, HALF)
         quantise_x(1, grouped_x[1])
         input_and_candidate(0, HALF, BANK)
+        c_bank = sum_of_rows(c_rows, first_rows, HID_BLOCKS)
         x_bank[3] = transpose_words(raw_x[3], back_bank())
         quantise_w(1, grouped_w[1])
         multiply(0, 1)
         activate_gate(0, GATE_F, ACT.Sigmoid, "f")
         activate_gate(0, GATE_O, ACT.Sigmoid, "o")
-        w_bank[2] = transpose_words(raw_w[2], back_bank())
-        c_bank = sum_of_rows(c_rows, first_rows, HID_BLOCKS)
         grouped_x[2] = regroup(nc.vector.tensor_copy, x_bank[2])
+        c_start = const.tile([P, HID_BLOCKS], F32)
+        nc.vector.tensor_copy(out=c_start[:], in_=c_bank[:, 0:HID_BLOCKS])
         quantise_x(2, grouped_x[2])
         input_and_candidate(1, 0, HALF)
+        w_bank[2] = transpose_words(raw_w[2], back_bank())
         grouped_x[3] = regroup(nc.vector.tensor_copy, x_bank[3])
         quantise_x(3, grouped_x[3])
         input_and_candidate(1, HALF, BANK)
         multiply(1, 1)
         activate_gate(1, GATE_F, ACT.Sigmoid, "f")
         activate_gate(1, GATE_O, ACT.Sigmoid, "o")
-        c_start = const.tile([P, HID_BLOCKS], F32)
-        nc.vector.tensor_copy(out=c_start[:], in_=c_bank[:, 0:HID_BLOCKS])
         input_times_candidate(0)
         grouped_w[2] = regroup(nc.vector.tensor_copy, w_bank[2])
         new_cell_state(0)

@@ -270,14 +270,18 @@ def tile_rdecommunicationlstm_pa_kernel(
         idle_bank = back_bank()
         keep_clock_up(12)
         x_bank[0] = transpose_words(raw_x[0], work_bank())
+        keep_clock_up(2)
         grouped_x[0] = regroup(nc.scalar.copy, x_bank[0])
         w_bank[0] = transpose_words(raw_w[0], work_bank())
+        keep_clock_up(2)
         grouped_w[0] = regroup(nc.scalar.copy, w_bank[0])
         quantise_x(0, grouped_x[0])
         x_bank[1] = transpose_words(raw_x[1], work_bank())
+        keep_clock_up(2)
         grouped_x[1] = regroup(nc.scalar.copy, x_bank[1])
         quantise_w(0, grouped_w[0])
         w_bank[1] = transpose_words(raw_w[1], work_bank())
+        keep_clock_up(2)
         grouped_w[1] = regroup(nc.scalar.copy, w_bank[1])
 
         def sum_of_rows(rows, which, columns):

@@ -268,20 +268,20 @@ def tile_rdecommunicationlstm_pa_kernel(
                 )
 
         idle_bank = back_bank()
-        keep_clock_up(12)
+        keep_clock_up(16)
         x_bank[0] = transpose_words(raw_x[0], work_bank())
-        keep_clock_up(2)
+        keep_clock_up(3)
         grouped_x[0] = regroup(nc.scalar.copy, x_bank[0])
         w_bank[0] = transpose_words(raw_w[0], work_bank())
-        keep_clock_up(2)
+        keep_clock_up(3)
         grouped_w[0] = regroup(nc.scalar.copy, w_bank[0])
         quantise_x(0, grouped_x[0])
         x_bank[1] = transpose_words(raw_x[1], work_bank())
-        keep_clock_up(2)
+        keep_clock_up(3)
         grouped_x[1] = regroup(nc.scalar.copy, x_bank[1])
         quantise_w(0, grouped_w[0])
         w_bank[1] = transpose_words(raw_w[1], work_bank())
-        keep_clock_up(2)
+        keep_clock_up(3)
         grouped_w[1] = regroup(nc.scalar.copy, w_bank[1])
 
         def sum_of_rows(rows, which, columns):
@@ -296,6 +296,7 @@ def tile_rdecommunicationlstm_pa_kernel(
         nc.vector.tensor_copy(out=bias[:], in_=bias_bank[:, 0:VECTOR_ROWS])
 
         x_bank[2] = transpose_words(raw_x[2], back_bank())
+        keep_clock_up(3)
         input_and_candidate(0, 0, HALF)
         quantise_x(1, grouped_x[1])
         input_and_candidate(0, HALF, BANK)

@@ -268,7 +268,7 @@ def tile_rdecommunicationlstm_pa_kernel(
                 )
 
         idle_bank = back_bank()
-        keep_clock_up(16)
+        keep_clock_up(14)
         x_bank[0] = transpose_words(raw_x[0], work_bank())
         keep_clock_up(3)
         grouped_x[0] = regroup(nc.scalar.copy, x_bank[0])
@@ -281,7 +281,7 @@ def tile_rdecommunicationlstm_pa_kernel(
         grouped_x[1] = regroup(nc.scalar.copy, x_bank[1])
         quantise_w(0, grouped_w[0])
         w_bank[1] = transpose_words(raw_w[1], work_bank())
-        keep_clock_up(3)
+        keep_clock_up(2)
         grouped_w[1] = regroup(nc.scalar.copy, w_bank[1])
 
         def sum_of_rows(rows, which, columns):
@@ -296,7 +296,6 @@ def tile_rdecommunicationlstm_pa_kernel(
         nc.vector.tensor_copy(out=bias[:], in_=bias_bank[:, 0:VECTOR_ROWS])
 
         x_bank[2] = transpose_words(raw_x[2], back_bank())
-        keep_clock_up(3)
         input_and_candidate(0, 0, HALF)
         quantise_x(1, grouped_x[1])
         input_and_candidate(0, HALF, BANK)

@@ -54,21 +54,22 @@ def tile_rdecommunicationlstm_pa_kernel(
                 in_=vec.rearrange("(r c) -> r c", c=P),
             )
 
-        nc.scalar.dma_start(out=c_rows[0:HID_BLOCKS, :], in_=c_init.rearrange("(r c) -> r c", c=P))
-
         x_rows = regime_vector.rearrange("(n p c a) k -> n c p a k", n=HALVES, p=P, a=2)
         w_rows = W_ih0.rearrange("(h e j p) k -> j e p h k", h=2, e=2, p=P)
 
         def load(rows):
-            raw = raw_pool.tile([P, 2 * K], BF16, tag="raw")
+            raw = raw_pool.tile([P, 2 * K], BF16, tag="raw", name="raw")
             nc.sync.dma_start(out=raw[:].rearrange("p (a k) -> p a k", a=2), in_=rows)
             return raw
 
-        raw_x = {}
-        raw_w = {}
-        for piece in (0, 1):
-            raw_x[piece] = load(x_rows[piece // 2, piece % 2])
-            raw_w[piece] = load(w_rows[0, piece])
+        raw_x = {0: raw_pool.tile([P, 2 * K], BF16, tag="raw", name="raw")}
+        raw_w = {0: raw_pool.tile([P, 2 * K], BF16, tag="raw", name="raw")}
+        for raw, rows in ((raw_x[0], x_rows[0, 0]), (raw_w[0], w_rows[0, 0])):
+            for a in range(2):
+                nc.sync.dma_start(out=raw[:, a * K : (a + 1) * K], in_=rows[:, a])
+        raw_x[1] = load(x_rows[0, 1])
+        raw_w[1] = load(w_rows[0, 1])
+        nc.sync.dma_start(out=c_rows[0:HID_BLOCKS, :], in_=c_init.rearrange("(r c) -> r c", c=P))
         for c in (2, 3):
             raw_x[c] = load(x_rows[c // 2, c % 2])
         for w in range(2, W_PIECES):
@@ -268,7 +269,7 @@ def tile_rdecommunicationlstm_pa_kernel(
                 )
 
         idle_bank = back_bank()
-        keep_clock_up(14)
+        keep_clock_up(13)
         x_bank[0] = transpose_words(raw_x[0], work_bank())
         keep_clock_up(3)
         grouped_x[0] = regroup(nc.scalar.copy, x_bank[0])

from contextlib import ExitStack

import concourse.mybir as mybir
from concourse.masks import make_identity

F32 = mybir.dt.float32
BF16 = mybir.dt.bfloat16
U32 = mybir.dt.uint32
U8 = mybir.dt.uint8
FP8X4 = mybir.dt.float8_e4m3fn_x4
ACT = mybir.ActivationFunctionType
ALU = mybir.AluOpType

P = 128
BATCH, K, HID, GATES = 1024, 512, 1024, 4
PACK = 4
BANK = 512
PIECE = 2 * P
X_PIECES = BATCH // PIECE
W_PIECES = GATES * HID // PIECE
HID_BLOCKS = HID // P
HALVES = BATCH // BANK
UNITS = HID_BLOCKS * HALVES
GATE_I, GATE_F, GATE_G, GATE_O = 0, 1, 2, 3
VECTOR_ROWS = GATES * HID // P
HALF = BANK // 2
LAST_UNIT_PARTS = (2 * P, P, P)

FLOPS = 2 * BATCH * GATES * HID * K


def tile_rdecommunicationlstm_pa_kernel(
    tc, regime_vector, W_ih0, hh_gates, b_ih0, b_hh0, c_init, out
):
    nc = tc.nc
    with ExitStack() as ctx:
        const = ctx.enter_context(tc.tile_pool(name="const", bufs=1))
        raw_pool = ctx.enter_context(tc.tile_pool(name="raw", bufs=X_PIECES + W_PIECES))
        grouped_pool = ctx.enter_context(tc.tile_pool(name="grouped", bufs=4))
        w_mx_pool = ctx.enter_context(tc.tile_pool(name="w_mx", bufs=W_PIECES))
        cell_pool = ctx.enter_context(tc.tile_pool(name="cell", bufs=4))
        psum = ctx.enter_context(tc.psum_pool(name="psum", bufs=1))
        ctx.enter_context(tc.manual_schedule())

        zeros = const.tile([P, P], BF16)
        nc.vector.memset(zeros[:], 0.0)
        vector_rows = const.tile([P, P], BF16)
        nc.vector.memset(vector_rows[3 * VECTOR_ROWS : P, :], 0.0)
        c_rows = const.tile([P, P], BF16)
        nc.vector.memset(c_rows[:], 0.0)
        for slot, vec in enumerate((hh_gates, b_ih0, b_hh0)):
            nc.scalar.dma_start(
                out=vector_rows[slot * VECTOR_ROWS : (slot + 1) * VECTOR_ROWS, :],
                in_=vec.rearrange("(r c) -> r c", c=P),
            )

        x_rows = regime_vector.rearrange("(n p c a) k -> n c p a k", n=HALVES, p=P, a=2)
        w_rows = W_ih0.rearrange("(h e j p) k -> j e p h k", h=2, e=2, p=P)

        def load(rows):
            raw = raw_pool.tile([P, 2 * K], BF16, tag="raw", name="raw")
            nc.sync.dma_start(out=raw[:].rearrange("p (a k) -> p a k", a=2), in_=rows)
            return raw

        raw_x = {0: raw_pool.tile([P, 2 * K], BF16, tag="raw", name="raw")}
        raw_w = {0: raw_pool.tile([P, 2 * K], BF16, tag="raw", name="raw")}
        for raw, rows in ((raw_x[0], x_rows[0, 0]), (raw_w[0], w_rows[0, 0])):
            for a in range(2):
                nc.sync.dma_start(out=raw[:, a * K : (a + 1) * K], in_=rows[:, a])
        raw_x[1] = load(x_rows[0, 1])
        raw_w[1] = load(w_rows[0, 1])
        nc.sync.dma_start(out=c_rows[0:HID_BLOCKS, :], in_=c_init.rearrange("(r c) -> r c", c=P))
        for c in (2, 3):
            raw_x[c] = load(x_rows[c // 2, c % 2])
        for w in range(2, W_PIECES):
            raw_w[w] = load(w_rows[w // 2, w % 2])

        ident = const.tile([P, P], F32)
        make_identity(nc, ident[:])
        warm_in = const.tile([P, 1], F32)
        warm_out = const.tile([P, 1], F32)
        nc.vector.memset(warm_in[:], 0.0)
        nc.scalar.activation(out=warm_out[:], in_=warm_in[:], func=ACT.Sigmoid)

        select = const.tile([P, VECTOR_ROWS], BF16)
        first_rows = const.tile([P, HID_BLOCKS], BF16)
        two_slots = const.tile([P, VECTOR_ROWS], F32)
        nc.vector.tensor_tensor(
            out=two_slots[:],
            in0=ident[:, 0:VECTOR_ROWS],
            in1=ident[:, VECTOR_ROWS : 2 * VECTOR_ROWS],
            op=ALU.add,
        )
        nc.vector.tensor_copy(out=first_rows[:], in_=ident[:, 0:HID_BLOCKS])
        nc.vector.tensor_tensor(
            out=select[:],
            in0=two_slots[:],
            in1=ident[:, 2 * VECTOR_ROWS : 3 * VECTOR_ROWS],
            op=ALU.add,
        )

        x_codes = const.tile([P, BATCH], U32, align_bytes=64)
        x_scales = const.tile([P, BATCH], U8, align_bytes=64)

        def work_bank():
            return psum.tile([P, BANK], F32, tag="work", bufs=5, name="work")

        def back_bank():
            return psum.tile([P, BANK], F32, tag="back", bufs=3, name="back")

        def transpose_words(raw, bank):
            words = raw[:].bitcast(F32)
            for s in range(BANK // P):
                a, u = divmod(s, 2)
                nc.tensor.transpose(
                    out=bank[:, s * P : (s + 1) * P],
                    in_=words[:, a * PIECE + u : (a + 1) * PIECE : 2],
                    identity=ident[:],
                )
            return bank

        def regroup(copy, bank):
            grouped = grouped_pool.tile([P, PIECE * PACK], BF16, tag="grouped", align_bytes=64)
            copy(
                out=grouped[:].bitcast(F32).rearrange("p (a r u) -> p a r u", a=2, u=2),
                in_=bank[:].rearrange("p (a u r) -> p a r u", a=2, u=2),
            )
            return grouped

        def quantise(grouped, codes, scales):
            nc.vector.quantize_mx(out=codes.bitcast(FP8X4), scales=scales, in_=grouped[:])

        def quantise_x(c, grouped):
            cols = slice(c * PIECE, (c + 1) * PIECE)
            quantise(grouped, x_codes[:, cols], x_scales[:, cols])

        w_mx = {}

        def quantise_w(w, grouped):
            w_codes = w_mx_pool.tile([P, PIECE], U32, tag="w_codes", align_bytes=64)
            w_scales = w_mx_pool.tile([P, PIECE], U8, tag="w_scales", align_bytes=64)
            quantise(grouped, w_codes[:], w_scales[:])
            w_mx[w] = (w_codes, w_scales)

        gate_bank = {}
        cell = {}

        def multiply(unit, e, lo=0, hi=BANK):
            j, n = divmod(unit, HALVES)
            w_codes, w_scales = w_mx[2 * j + e]
            batch = slice(n * BANK + lo, n * BANK + hi)
            for h in range(2):
                hidden = slice(h * P, (h + 1) * P)
                bank = work_bank()
                nc.tensor.matmul_mx(
                    out=bank[:, lo:hi],
                    lhsT=w_codes[:, hidden].bitcast(FP8X4),
                    lhsT_scale=w_scales[:, hidden],
                    rhs=x_codes[:, batch].bitcast(FP8X4),
                    rhs_scale=x_scales[:, batch],
                    start=True,
                    stop=True,
                )
                gate_bank[unit, 2 * h + e, lo] = bank

        def activate_gate(unit, gate, func, name, lo=0, hi=BANK):
            j = unit // HALVES
            col = gate * HID_BLOCKS + j
            if lo == 0:
                cell[unit, name] = cell_pool.tile([P, BANK], F32, tag=name, name=name)
            nc.scalar.activation(
                out=cell[unit, name][:, lo:hi],
                in_=gate_bank[unit, gate, lo if (unit, gate, lo) in gate_bank else 0][:, lo:hi],
                func=func,
                bias=bias[:, col : col + 1],
            )

        def parts_of(unit):
            parts = []
            lo = 0
            for width in LAST_UNIT_PARTS if unit == UNITS - 1 else (BANK,):
                parts.append((lo, lo + width))
                lo += width
            return parts

        def halves_of(unit):
            return [(0, HALF), (HALF, BANK)] if unit == UNITS - 1 else [(0, BANK)]

        def input_times_candidate(unit):
            ig = cell_pool.tile([P, BANK], F32, tag="ig")
            for lo, hi in halves_of(unit):
                nc.vector.tensor_tensor(
                    out=ig[:, lo:hi],
                    in0=cell[unit, "i"][:, lo:hi],
                    in1=cell[unit, "g"][:, lo:hi],
                    op=ALU.mult,
                )
            cell[unit, "ig"] = ig

        def new_cell_state(unit):
            j = unit // HALVES
            c_new = cell_pool.tile([P, BANK], F32, tag="c_new")
            for lo, hi in parts_of(unit):
                nc.vector.scalar_tensor_tensor(
                    out=c_new[:, lo:hi],
                    in0=cell[unit, "f"][:, lo:hi],
                    scalar=c_start[:, j : j + 1],
                    in1=cell[unit, "ig"][:, lo:hi],
                    op0=ALU.mult,
                    op1=ALU.add,
                )
            cell[unit, "c_new"] = c_new

        def batch_onto_partitions(unit, name, lo, hi, bank):
            for first in range(lo, hi, P):
                block = slice(first, first + P)
                nc.tensor.transpose(
                    out=bank[:, block], in_=cell[unit, name][:, block], identity=ident[:]
                )
            return bank

        def way_back(unit):
            bank = work_bank if unit == UNITS - 1 else back_bank
            for lo, hi in parts_of(unit):
                cell[unit, "c_T", lo] = batch_onto_partitions(unit, "c_new", lo, hi, bank())
            for lo, hi in halves_of(unit):
                cell[unit, "o_T", lo] = batch_onto_partitions(unit, "o", lo, hi, bank())

        def tanh_of_cell_state(unit):
            tanh_c = cell_pool.tile([P, BANK], F32, tag="tanh_c")
            for lo, hi in parts_of(unit):
                nc.scalar.activation(
                    out=tanh_c[:, lo:hi], in_=cell[unit, "c_T", lo][:, lo:hi], func=ACT.Tanh
                )
            cell[unit, "tanh_c"] = tanh_c

        out_blocks = out.rearrange("(n p t) (j c) -> n j p t c", t=BANK // P, p=P, c=P)

        def hidden_state(unit):
            j, n = divmod(unit, HALVES)
            h_new = cell_pool.tile([P, BANK], F32, tag="h_new")
            for lo, hi in parts_of(unit):
                half = max(start for start, stop in halves_of(unit) if start <= lo)
                nc.vector.tensor_tensor(
                    out=h_new[:, lo:hi],
                    in0=cell[unit, "o_T", half][:, lo:hi],
                    in1=cell[unit, "tanh_c"][:, lo:hi],
                    op=ALU.mult,
                )
                nc.sync.dma_start(
                    out=out_blocks[n, j, :, lo // P : hi // P, :],
                    in_=h_new[:, lo:hi].rearrange("p (t c) -> p t c", c=P),
                )

        grouped_x = {}
        grouped_w = {}
        x_bank = {}
        w_bank = {}

        def input_and_candidate(unit, lo, hi):
            multiply(unit, 0, lo, hi)
            activate_gate(unit, GATE_I, ACT.Sigmoid, "i", lo, hi)
            activate_gate(unit, GATE_G, ACT.Tanh, "g", lo, hi)

        def keep_clock_up(times):
            for i in range(times):
                nc.tensor.matmul(
                    out=idle_bank[:, 0:P], lhsT=zeros[:], rhs=zeros[:], start=True, stop=True
                )

        idle_bank = back_bank()
        keep_clock_up(13)
        x_bank[0] = transpose_words(raw_x[0], work_bank())
        keep_clock_up(3)
        grouped_x[0] = regroup(nc.scalar.copy, x_bank[0])
        w_bank[0] = transpose_words(raw_w[0], work_bank())
        keep_clock_up(3)
        grouped_w[0] = regroup(nc.scalar.copy, w_bank[0])
        quantise_x(0, grouped_x[0])
        x_bank[1] = transpose_words(raw_x[1], work_bank())
        keep_clock_up(3)
        grouped_x[1] = regroup(nc.scalar.copy, x_bank[1])
        quantise_w(0, grouped_w[0])
        w_bank[1] = transpose_words(raw_w[1], work_bank())
        keep_clock_up(2)
        grouped_w[1] = regroup(nc.scalar.copy, w_bank[1])

        def sum_of_rows(rows, which, columns):
            bank = back_bank()
            nc.tensor.matmul(
                out=bank[:, 0:columns], lhsT=rows[:], rhs=which[:], start=True, stop=True
            )
            return bank

        bias_bank = sum_of_rows(vector_rows, select, VECTOR_ROWS)
        bias = const.tile([P, VECTOR_ROWS], F32)
        nc.vector.tensor_copy(out=bias[:], in_=bias_bank[:, 0:VECTOR_ROWS])

        x_bank[2] = transpose_words(raw_x[2], back_bank())
        input_and_candidate(0, 0, HALF)
        quantise_x(1, grouped_x[1])
        input_and_candidate(0, HALF, BANK)
        c_bank = sum_of_rows(c_rows, first_rows, HID_BLOCKS)
        x_bank[3] = transpose_words(raw_x[3], back_bank())
        quantise_w(1, grouped_w[1])
        multiply(0, 1)
        activate_gate(0, GATE_F, ACT.Sigmoid, "f")
        activate_gate(0, GATE_O, ACT.Sigmoid, "o")
        grouped_x[2] = regroup(nc.vector.tensor_copy, x_bank[2])
        c_start = const.tile([P, HID_BLOCKS], F32)
        nc.vector.tensor_copy(out=c_start[:], in_=c_bank[:, 0:HID_BLOCKS])
        quantise_x(2, grouped_x[2])
        input_and_candidate(1, 0, HALF)
        w_bank[2] = transpose_words(raw_w[2], back_bank())
        grouped_x[3] = regroup(nc.vector.tensor_copy, x_bank[3])
        quantise_x(3, grouped_x[3])
        input_and_candidate(1, HALF, BANK)
        multiply(1, 1)
        activate_gate(1, GATE_F, ACT.Sigmoid, "f")
        activate_gate(1, GATE_O, ACT.Sigmoid, "o")
        input_times_candidate(0)
        grouped_w[2] = regroup(nc.vector.tensor_copy, w_bank[2])
        new_cell_state(0)
        quantise_w(2, grouped_w[2])
        w_bank[3] = transpose_words(raw_w[3], back_bank())
        multiply(2, 0)
        way_back(0)
        grouped_w[3] = regroup(nc.vector.tensor_copy, w_bank[3])
        w_bank[4] = transpose_words(raw_w[4], work_bank())
        input_times_candidate(1)
        quantise_w(3, grouped_w[3])
        new_cell_state(1)
        multiply(2, 1)
        grouped_w[4] = regroup(nc.vector.tensor_copy, w_bank[4])
        way_back(1)

        for t in range(2, UNITS):
            activate_gate(t, GATE_I, ACT.Sigmoid, "i")
            activate_gate(t, GATE_G, ACT.Tanh, "g")
            if t == 2:
                tanh_of_cell_state(0)
            activate_gate(t, GATE_F, ACT.Sigmoid, "f")
            if t == UNITS - 1:
                tanh_of_cell_state(t - 1)
            for lo, hi in halves_of(t):
                activate_gate(t, GATE_O, ACT.Sigmoid, "o", lo, hi)
            if t < UNITS - 1:
                tanh_of_cell_state(t - 1)
            if t == 2:
                hidden_state(0)
            input_times_candidate(t)
            if t + 2 < W_PIECES:
                quantise_w(t + 2, grouped_w[t + 2])
            if t + 1 < UNITS:
                multiply(t + 1, 0)
            if t + 3 < W_PIECES:
                w_bank[t + 3] = transpose_words(raw_w[t + 3], work_bank())
            if t + 1 < UNITS:
                multiply(t + 1, 1)
            new_cell_state(t)
            way_back(t)
            if t + 3 < W_PIECES:
                grouped_w[t + 3] = regroup(nc.vector.tensor_copy, w_bank[t + 3])
            hidden_state(t - 1)
        tanh_of_cell_state(UNITS - 1)
        hidden_state(UNITS - 1)
